import numpy as np
import ml_dtypes


def mxq(x, axis, fmt="e4m3"):
    dtype, down = {"e4m3": (ml_dtypes.float8_e4m3fn, 7), "e5m2": (ml_dtypes.float8_e5m2, 14)}[fmt]
    v = np.moveaxis(np.asarray(x, np.float32).astype(ml_dtypes.bfloat16).astype(np.float64), axis, -1)
    blocks = v.reshape(v.shape[:-1] + (-1, 32))
    amax = np.abs(blocks).max(-1, keepdims=True)
    byte = np.maximum(np.where(amax > 0, np.frexp(amax)[1] - 1 + 127, 0) - down, 1)
    scale = np.exp2(byte - 127.0)
    codes = (blocks / scale).astype(np.float32).astype(dtype).astype(np.float64)
    return np.moveaxis((codes * scale).reshape(v.shape), -1, axis)


WIDE = False


def mx_kscale(k):
    if not WIDE:
        return np.ones(k)
    levels = np.array([10, -10, 5, -5, 0])
    a = np.random.permutation(np.resize(levels, k // 512 * 4)).reshape(k // 512, 4)
    idx = np.arange(k)
    return np.exp2(a[idx // 512, idx % 128 // 32])


BF16 = ml_dtypes.bfloat16


def bf(x):
    return np.asarray(x, np.float32).astype(BF16)


def f64(x):
    return np.asarray(x).astype(np.float64)


B, N, D, O, M = 16, 512, 128, 512, 4


def setup_inputs():
    s = mx_kscale(N)
    t = s / s.min()
    eye = np.eye(N)
    adj = np.exp(2.0 * np.random.standard_normal((N, N)) - 2.0) * (3.0 / N)
    adj = (t * t)[:, None] * (adj + eye) - eye
    return {"inputs": bf(np.random.standard_normal((B, N, D)) / s[None, :, None]), "adj": bf(adj)}


def reference(inputs, adj):
    x0 = f64(inputs)
    m = f64(adj) + np.eye(N)
    d = m.sum(axis=1) ** -0.5
    support = (m * d[None, :]).T * d[None, :]
    sq = mxq(support, 1, "e4m3")
    x1 = sq @ mxq(x0, 1, "e4m3")
    x2 = 2.0 * (sq @ mxq(x1, 1, "e4m3")) - x0
    return x1, x2

@@ -1,0 +1,165 @@
+from contextlib import ExitStack
+
+import concourse.mybir as mybir
+from concourse.masks import make_identity
+
+F32 = mybir.dt.float32
+BF16 = mybir.dt.bfloat16
+U32 = mybir.dt.uint32
+U8 = mybir.dt.uint8
+FP8X4 = mybir.dt.float8_e4m3fn_x4
+ALU = mybir.AluOpType
+
+P = 128
+PACK = 4
+BATCH = 16
+NODES = P * PACK
+FEAT = 128
+FLOPS = 2 * 2 * BATCH * NODES * NODES * FEAT
+
+LOAD_BATCHES = 4
+RUN = 4
+SCALAR_X = BATCH // 2
+X_AHEAD = 2
+LAG = 2
+X1_BANKS = 4
+X2_BANKS = 3
+STAGE_BUFS = 8
+
+
+def tile_dgcn_pa_t_kernel(tc, inputs, adj, out_0, out_1):
+    nc = tc.nc
+    with ExitStack() as ctx:
+        ctx.enter_context(tc.manual_schedule())
+        keep = ctx.enter_context(tc.tile_pool(name="keep", bufs=1))
+        stage = ctx.enter_context(tc.tile_pool(name="stage", bufs=STAGE_BUFS))
+        psum = ctx.enter_context(tc.psum_pool(name="psum", bufs=1))
+
+        adj_raw = keep.tile([P, PACK, NODES], BF16)
+        adj_rows = adj.rearrange("(p t) i -> p t i", t=PACK)
+        for t in range(PACK):
+            nc.sync.dma_start(out=adj_raw[:, t, :], in_=adj_rows[:, t, :])
+        x_raw = keep.tile([P, BATCH, PACK, FEAT], BF16)
+        for b in range(0, BATCH, LOAD_BATCHES):
+            nc.sync.dma_start(
+                out=x_raw[:, b : b + LOAD_BATCHES],
+                in_=inputs[b : b + LOAD_BATCHES].rearrange("b (p t) d -> p b t d", t=PACK),
+            )
+
+        ident = keep.tile([P, P], F32)
+        make_identity(nc, ident[:])
+        eye = keep.tile([P, PACK, P, PACK], BF16)
+        nc.vector.memset(eye[:], 0.0)
+        for t in range(PACK):
+            nc.vector.tensor_copy(out=eye[:, t, :, t], in_=ident[:])
+
+        m = keep.tile([P, PACK, NODES], F32)
+        row_sum = keep.tile([P, PACK], F32)
+        for t in range(PACK):
+            nc.vector.scalar_tensor_tensor(
+                out=m[:, t, :],
+                in0=adj_raw[:, t, :],
+                scalar=1.0,
+                in1=eye[:, t].rearrange("p q u -> p (q u)"),
+                op0=ALU.mult,
+                op1=ALU.add,
+                accum_out=row_sum[:, t : t + 1],
+            )
+        inv_sum = keep.tile([P, PACK], F32)
+        nc.vector.reciprocal(inv_sum[:], row_sum[:])
+        dd = keep.tile([P, PACK], F32)
+        nc.scalar.sqrt(dd[:], inv_sum[:])
+        dd_row = psum.tile([P, PACK, P], F32)
+        for u in range(PACK):
+            nc.tensor.transpose(dd_row[:, u, :], dd[:, u : u + 1].to_broadcast([P, P]), ident[:])
+        m_scaled = keep.tile([P, PACK, NODES], F32)
+        for t in range(PACK):
+            nc.vector.tensor_scalar_mul(out=m_scaled[:, t, :], in0=m[:, t, :], scalar1=dd[:, t : t + 1])
+        s_grouped = keep.tile([P, PACK, P, PACK], BF16, align_bytes=64)
+        nc.vector.tensor_tensor(
+            out=s_grouped[:],
+            in0=m_scaled[:].rearrange("p t (q u) -> p u q t", u=PACK),
+            in1=dd_row[:].unsqueeze(3).to_broadcast([P, PACK, P, PACK]),
+            op=ALU.mult,
+        )
+        s_codes = keep.tile([P, PACK, P], U32, align_bytes=64)
+        s_scales = keep.tile([P, PACK, P], U8, align_bytes=64)
+        nc.vector.quantize_mx(
+            out=s_codes[:].rearrange("p u q -> p (u q)").bitcast(FP8X4),
+            scales=s_scales[:].rearrange("p u q -> p (u q)"),
+            in_=s_grouped[:].rearrange("p u q t -> p (u q t)"),
+        )
+
+        x_grouped = keep.tile([P, BATCH, FEAT, PACK], BF16, align_bytes=64)
+        x_codes = keep.tile([P, BATCH, FEAT], U32, align_bytes=64)
+        x_scales = keep.tile([P, BATCH, FEAT], U8, align_bytes=64)
+
+        def regroup_x(copy, b):
+            copy(
+                out=x_grouped[:, b].rearrange("p (c i) t -> p c t i", i=RUN),
+                in_=x_raw[:, b].rearrange("p t (c i) -> p c t i", i=RUN),
+            )
+
+        def quantise_x(b):
+            nc.vector.quantize_mx(
+                out=x_codes[:, b, :].bitcast(FP8X4),
+                scales=x_scales[:, b, :],
+                in_=x_grouped[:, b].rearrange("p d t -> p (d t)"),
+            )
+
+        x1_grouped = keep.tile([P, BATCH, FEAT, PACK], BF16, align_bytes=64)
+        x1_codes = keep.tile([P, BATCH, FEAT], U32, align_bytes=64)
+        x1_scales = keep.tile([P, BATCH, FEAT], U8, align_bytes=64)
+
+        def multiply_by_support(bank, codes, scales):
+            for u in range(PACK):
+                nc.tensor.matmul_mx(
+                    out=bank[:, u, :],
+                    lhsT=s_codes[:, u, :].bitcast(FP8X4),
+                    lhsT_scale=s_scales[:, u, :],
+                    rhs=codes.bitcast(FP8X4),
+                    rhs_scale=scales,
+                    start=True,
+                    stop=True,
+                )
+
+        def first_product(b):
+            x1_bank = psum.tile([P, PACK, FEAT], F32, bufs=X1_BANKS)
+            multiply_by_support(x1_bank, x_codes[:, b, :], x_scales[:, b, :])
+            x1_out = stage.tile([P, PACK, FEAT], F32)
+            nc.scalar.copy(out=x1_out[:], in_=x1_bank[:])
+            nc.sync.dma_start(out=out_0[b].rearrange("(q u) d -> q u d", u=PACK), in_=x1_out[:])
+            nc.scalar.copy(out=x1_grouped[:, b], in_=x1_bank[:].rearrange("q u d -> q d u"))
+
+        def second_product(b):
+            nc.vector.quantize_mx(
+                out=x1_codes[:, b, :].bitcast(FP8X4),
+                scales=x1_scales[:, b, :],
+                in_=x1_grouped[:, b].rearrange("q d u -> q (d u)"),
+            )
+            x2_bank = psum.tile([P, PACK, FEAT], F32, bufs=X2_BANKS)
+            multiply_by_support(x2_bank, x1_codes[:, b, :], x1_scales[:, b, :])
+            x2_out = stage.tile([P, PACK, FEAT], F32)
+            nc.vector.scalar_tensor_tensor(
+                out=x2_out[:],
+                in0=x2_bank[:],
+                scalar=2.0,
+                in1=x_raw[:, b],
+                op0=ALU.mult,
+                op1=ALU.subtract,
+            )
+            nc.sync.dma_start(out=out_1[b].rearrange("(q u) d -> q u d", u=PACK), in_=x2_out[:])
+
+        for b in range(SCALAR_X):
+            regroup_x(nc.scalar.copy, b)
+        for b in range(X_AHEAD):
+            quantise_x(b)
+        for b in range(BATCH + LAG):
+            if b + SCALAR_X < BATCH:
+                regroup_x(nc.vector.tensor_copy, b + SCALAR_X)
+            if b + X_AHEAD < BATCH:
+                quantise_x(b + X_AHEAD)
+            if b < BATCH:
+                first_product(b)
+            if b >= LAG:
+                second_product(b - LAG)

@@ -21,7 +21,8 @@ LOAD_BATCHES = 4
 RUN = 4
 SCALAR_X = BATCH // 2
 X_AHEAD = 2
-LAG = 2
+QUANT_LAG = 2
+OUT_LAG = 3
 X1_BANKS = 4
 X2_BANKS = 3
 STAGE_BUFS = 8
@@ -131,6 +132,8 @@ def tile_dgcn_pa_t_kernel(tc, inputs, adj, out_0, out_1):
             nc.sync.dma_start(out=out_0[b].rearrange("(q u) d -> q u d", u=PACK), in_=x1_out[:])
             nc.scalar.copy(out=x1_grouped[:, b], in_=x1_bank[:].rearrange("q u d -> q d u"))
 
+        x2_banks = {}
+
         def second_product(b):
             nc.vector.quantize_mx(
                 out=x1_codes[:, b, :].bitcast(FP8X4),
@@ -139,10 +142,13 @@ def tile_dgcn_pa_t_kernel(tc, inputs, adj, out_0, out_1):
             )
             x2_bank = psum.tile([P, PACK, FEAT], F32, bufs=X2_BANKS)
             multiply_by_support(x2_bank, x1_codes[:, b, :], x1_scales[:, b, :])
+            x2_banks[b] = x2_bank
+
+        def finish_x2(b):
             x2_out = stage.tile([P, PACK, FEAT], F32)
             nc.vector.scalar_tensor_tensor(
                 out=x2_out[:],
-                in0=x2_bank[:],
+                in0=x2_banks[b][:],
                 scalar=2.0,
                 in1=x_raw[:, b],
                 op0=ALU.mult,
@@ -154,12 +160,14 @@ def tile_dgcn_pa_t_kernel(tc, inputs, adj, out_0, out_1):
             regroup_x(nc.scalar.copy, b)
         for b in range(X_AHEAD):
             quantise_x(b)
-        for b in range(BATCH + LAG):
+        for b in range(BATCH + OUT_LAG):
+            if b < BATCH:
+                first_product(b)
+            if QUANT_LAG <= b < BATCH + QUANT_LAG:
+                second_product(b - QUANT_LAG)
+            if b >= OUT_LAG:
+                finish_x2(b - OUT_LAG)
             if b + SCALAR_X < BATCH:
                 regroup_x(nc.vector.tensor_copy, b + SCALAR_X)
             if b + X_AHEAD < BATCH:
                 quantise_x(b + X_AHEAD)
-            if b < BATCH:
-                first_product(b)
-            if b >= LAG:
-                second_product(b - LAG)

@@ -9,6 +9,7 @@ U32 = mybir.dt.uint32
 U8 = mybir.dt.uint8
 FP8X4 = mybir.dt.float8_e4m3fn_x4
 ALU = mybir.AluOpType
+ACT = mybir.ActivationFunctionType
 
 P = 128
 PACK = 4
@@ -19,7 +20,7 @@ FLOPS = 2 * 2 * BATCH * NODES * NODES * FEAT
 
 LOAD_BATCHES = 4
 RUN = 4
-SCALAR_X = BATCH // 2
+SCALAR_X = 7
 X_AHEAD = 2
 QUANT_LAG = 2
 OUT_LAG = 3
@@ -47,6 +48,11 @@ def tile_dgcn_pa_t_kernel(tc, inputs, adj, out_0, out_1):
                 in_=inputs[b : b + LOAD_BATCHES].rearrange("b (p t) d -> p b t d", t=PACK),
             )
 
+        one = keep.tile([P, 1], F32)
+        nc.vector.memset(one[:], 1.0)
+        warm = keep.tile([P, 1], F32)
+        nc.scalar.activation(out=warm[:], in_=one[:], func=ACT.Abs_reciprocal_sqrt)
+
         ident = keep.tile([P, P], F32)
         make_identity(nc, ident[:])
         eye = keep.tile([P, PACK, P, PACK], BF16)
@@ -56,7 +62,8 @@ def tile_dgcn_pa_t_kernel(tc, inputs, adj, out_0, out_1):
 
         m = keep.tile([P, PACK, NODES], F32)
         row_sum = keep.tile([P, PACK], F32)
-        for t in range(PACK):
+        unused = keep.tile([P, NODES], BF16)
+        for t in range(0, PACK, 2):
             nc.vector.scalar_tensor_tensor(
                 out=m[:, t, :],
                 in0=adj_raw[:, t, :],
@@ -66,15 +73,23 @@ def tile_dgcn_pa_t_kernel(tc, inputs, adj, out_0, out_1):
                 op1=ALU.add,
                 accum_out=row_sum[:, t : t + 1],
             )
-        inv_sum = keep.tile([P, PACK], F32)
-        nc.vector.reciprocal(inv_sum[:], row_sum[:])
+        for t in range(1, PACK, 2):
+            nc.scalar.activation(
+                out=unused[:], in_=adj_raw[:, t, :], func=ACT.Copy, bias=1.0 / NODES, accum_out=row_sum[:, t : t + 1]
+            )
         dd = keep.tile([P, PACK], F32)
-        nc.scalar.sqrt(dd[:], inv_sum[:])
+        nc.scalar.activation(out=dd[:], in_=row_sum[:], func=ACT.Abs_reciprocal_sqrt)
+        for t in range(1, PACK, 2):
+            nc.vector.tensor_tensor(
+                out=m[:, t, :], in0=adj_raw[:, t, :], in1=eye[:, t].rearrange("p q u -> p (q u)"), op=ALU.add
+            )
         dd_row = psum.tile([P, PACK, P], F32)
         for u in range(PACK):
             nc.tensor.transpose(dd_row[:, u, :], dd[:, u : u + 1].to_broadcast([P, P]), ident[:])
         m_scaled = keep.tile([P, PACK, NODES], F32)
-        for t in range(PACK):
+        for t in range(0, PACK, 2):
+            nc.scalar.activation(out=m_scaled[:, t, :], in_=m[:, t, :], func=ACT.Copy, scale=dd[:, t : t + 1])
+        for t in range(1, PACK, 2):
             nc.vector.tensor_scalar_mul(out=m_scaled[:, t, :], in0=m[:, t, :], scalar1=dd[:, t : t + 1])
         s_grouped = keep.tile([P, PACK, P, PACK], BF16, align_bytes=64)
         nc.vector.tensor_tensor(

@@ -21,8 +21,9 @@ FLOPS = 2 * 2 * BATCH * NODES * NODES * FEAT
 LOAD_BATCHES = 4
 RUN = 4
 SCALAR_X = 7
-X_AHEAD = 2
-QUANT_LAG = 2
+X_QUANT = 4
+X1_QUANT = 2
+QUANT_LAG = 1
 OUT_LAG = 3
 X1_BANKS = 4
 X2_BANKS = 3
@@ -116,11 +117,11 @@ def tile_dgcn_pa_t_kernel(tc, inputs, adj, out_0, out_1):
                 in_=x_raw[:, b].rearrange("p t (c i) -> p c t i", i=RUN),
             )
 
-        def quantise_x(b):
+        def quantise(codes, scales, grouped, b, count):
             nc.vector.quantize_mx(
-                out=x_codes[:, b, :].bitcast(FP8X4),
-                scales=x_scales[:, b, :],
-                in_=x_grouped[:, b].rearrange("p d t -> p (d t)"),
+                out=codes[:, b : b + count, :].rearrange("p b d -> p (b d)").bitcast(FP8X4),
+                scales=scales[:, b : b + count, :].rearrange("p b d -> p (b d)"),
+                in_=grouped[:, b : b + count].rearrange("p b d t -> p (b d t)"),
             )
 
         x1_grouped = keep.tile([P, BATCH, FEAT, PACK], BF16, align_bytes=64)
@@ -150,11 +151,6 @@ def tile_dgcn_pa_t_kernel(tc, inputs, adj, out_0, out_1):
         x2_banks = {}
 
         def second_product(b):
-            nc.vector.quantize_mx(
-                out=x1_codes[:, b, :].bitcast(FP8X4),
-                scales=x1_scales[:, b, :],
-                in_=x1_grouped[:, b].rearrange("q d u -> q (d u)"),
-            )
             x2_bank = psum.tile([P, PACK, FEAT], F32, bufs=X2_BANKS)
             multiply_by_support(x2_bank, x1_codes[:, b, :], x1_scales[:, b, :])
             x2_banks[b] = x2_bank
@@ -173,16 +169,23 @@ def tile_dgcn_pa_t_kernel(tc, inputs, adj, out_0, out_1):
 
         for b in range(SCALAR_X):
             regroup_x(nc.scalar.copy, b)
-        for b in range(X_AHEAD):
-            quantise_x(b)
+        quantise(x_codes, x_scales, x_grouped, 0, X_QUANT)
+        x1_groups = {}
+        for b in range(0, BATCH - X1_QUANT, X1_QUANT):
+            x1_groups[b + X1_QUANT - 1] = (b, X1_QUANT)
+        for b in range(BATCH - X1_QUANT, BATCH):
+            x1_groups[b] = (b, 1)
         for b in range(BATCH + OUT_LAG):
             if b < BATCH:
                 first_product(b)
-            if QUANT_LAG <= b < BATCH + QUANT_LAG:
-                second_product(b - QUANT_LAG)
             if b >= OUT_LAG:
                 finish_x2(b - OUT_LAG)
+            if b - QUANT_LAG in x1_groups:
+                first, count = x1_groups[b - QUANT_LAG]
+                quantise(x1_codes, x1_scales, x1_grouped, first, count)
+                for c in range(first, first + count):
+                    second_product(c)
             if b + SCALAR_X < BATCH:
                 regroup_x(nc.vector.tensor_copy, b + SCALAR_X)
-            if b + X_AHEAD < BATCH:
-                quantise_x(b + X_AHEAD)
+            if (b + SCALAR_X) % X_QUANT == 0 and X_QUANT < b + SCALAR_X <= BATCH:
+                quantise(x_codes, x_scales, x_grouped, b + SCALAR_X - X_QUANT, X_QUANT)

@@ -23,8 +23,9 @@ RUN = 4
 SCALAR_X = 7
 X_QUANT = 4
 X1_QUANT = 2
-QUANT_LAG = 1
-OUT_LAG = 3
+AHEAD = 2
+QUANT_LAG = 2
+OUT_LAG = 4
 X1_BANKS = 4
 X2_BANKS = 3
 STAGE_BUFS = 8
@@ -101,11 +102,6 @@ def tile_dgcn_pa_t_kernel(tc, inputs, adj, out_0, out_1):
         )
         s_codes = keep.tile([P, PACK, P], U32, align_bytes=64)
         s_scales = keep.tile([P, PACK, P], U8, align_bytes=64)
-        nc.vector.quantize_mx(
-            out=s_codes[:].rearrange("p u q -> p (u q)").bitcast(FP8X4),
-            scales=s_scales[:].rearrange("p u q -> p (u q)"),
-            in_=s_grouped[:].rearrange("p u q t -> p (u q t)"),
-        )
 
         x_grouped = keep.tile([P, BATCH, FEAT, PACK], BF16, align_bytes=64)
         x_codes = keep.tile([P, BATCH, FEAT], U32, align_bytes=64)
@@ -140,9 +136,15 @@ def tile_dgcn_pa_t_kernel(tc, inputs, adj, out_0, out_1):
                     stop=True,
                 )
 
+        x1_banks = {}
+
         def first_product(b):
             x1_bank = psum.tile([P, PACK, FEAT], F32, bufs=X1_BANKS)
             multiply_by_support(x1_bank, x_codes[:, b, :], x_scales[:, b, :])
+            x1_banks[b] = x1_bank
+
+        def take_x1(b):
+            x1_bank = x1_banks[b]
             x1_out = stage.tile([P, PACK, FEAT], F32)
             nc.scalar.copy(out=x1_out[:], in_=x1_bank[:])
             nc.sync.dma_start(out=out_0[b].rearrange("(q u) d -> q u d", u=PACK), in_=x1_out[:])
@@ -169,22 +171,32 @@ def tile_dgcn_pa_t_kernel(tc, inputs, adj, out_0, out_1):
 
         for b in range(SCALAR_X):
             regroup_x(nc.scalar.copy, b)
-        quantise(x_codes, x_scales, x_grouped, 0, X_QUANT)
+        quantise(x_codes, x_scales, x_grouped, 0, X_QUANT // 2)
+        nc.vector.quantize_mx(
+            out=s_codes[:].rearrange("p u q -> p (u q)").bitcast(FP8X4),
+            scales=s_scales[:].rearrange("p u q -> p (u q)"),
+            in_=s_grouped[:].rearrange("p u q t -> p (u q t)"),
+        )
+        quantise(x_codes, x_scales, x_grouped, X_QUANT // 2, X_QUANT // 2)
         x1_groups = {}
         for b in range(0, BATCH - X1_QUANT, X1_QUANT):
             x1_groups[b + X1_QUANT - 1] = (b, X1_QUANT)
         for b in range(BATCH - X1_QUANT, BATCH):
             x1_groups[b] = (b, 1)
+        for b in range(AHEAD):
+            first_product(b)
         for b in range(BATCH + OUT_LAG):
+            if b + AHEAD < BATCH:
+                first_product(b + AHEAD)
             if b < BATCH:
-                first_product(b)
-            if b >= OUT_LAG:
-                finish_x2(b - OUT_LAG)
+                take_x1(b)
             if b - QUANT_LAG in x1_groups:
                 first, count = x1_groups[b - QUANT_LAG]
                 quantise(x1_codes, x1_scales, x1_grouped, first, count)
                 for c in range(first, first + count):
                     second_product(c)
+            if b >= OUT_LAG:
+                finish_x2(b - OUT_LAG)
             if b + SCALAR_X < BATCH:
                 regroup_x(nc.vector.tensor_copy, b + SCALAR_X)
             if (b + SCALAR_X) % X_QUANT == 0 and X_QUANT < b + SCALAR_X <= BATCH:

@@ -20,12 +20,14 @@ FLOPS = 2 * 2 * BATCH * NODES * NODES * FEAT
 
 LOAD_BATCHES = 4
 RUN = 4
-SCALAR_X = 7
+SCALAR_X = 6
 X_QUANT = 4
 X1_QUANT = 2
 AHEAD = 2
 QUANT_LAG = 2
 OUT_LAG = 4
+EARLY = 4
+HALF = PACK // 2
 X1_BANKS = 4
 X2_BANKS = 3
 STAGE_BUFS = 8
@@ -94,14 +96,23 @@ def tile_dgcn_pa_t_kernel(tc, inputs, adj, out_0, out_1):
         for t in range(1, PACK, 2):
             nc.vector.tensor_scalar_mul(out=m_scaled[:, t, :], in0=m[:, t, :], scalar1=dd[:, t : t + 1])
         s_grouped = keep.tile([P, PACK, P, PACK], BF16, align_bytes=64)
-        nc.vector.tensor_tensor(
-            out=s_grouped[:],
-            in0=m_scaled[:].rearrange("p t (q u) -> p u q t", u=PACK),
-            in1=dd_row[:].unsqueeze(3).to_broadcast([P, PACK, P, PACK]),
-            op=ALU.mult,
-        )
         s_codes = keep.tile([P, PACK, P], U32, align_bytes=64)
         s_scales = keep.tile([P, PACK, P], U8, align_bytes=64)
+
+        def scale_columns(us):
+            nc.vector.tensor_tensor(
+                out=s_grouped[:, us],
+                in0=m_scaled[:].rearrange("p t (q u) -> p u q t", u=PACK)[:, us],
+                in1=dd_row[:, us].unsqueeze(3).to_broadcast([P, HALF, P, PACK]),
+                op=ALU.mult,
+            )
+
+        def quantise_support(us):
+            nc.vector.quantize_mx(
+                out=s_codes[:, us].rearrange("p u q -> p (u q)").bitcast(FP8X4),
+                scales=s_scales[:, us].rearrange("p u q -> p (u q)"),
+                in_=s_grouped[:, us].rearrange("p u q t -> p (u q t)"),
+            )
 
         x_grouped = keep.tile([P, BATCH, FEAT, PACK], BF16, align_bytes=64)
         x_codes = keep.tile([P, BATCH, FEAT], U32, align_bytes=64)
@@ -137,18 +148,43 @@ def tile_dgcn_pa_t_kernel(tc, inputs, adj, out_0, out_1):
                 )
 
         x1_banks = {}
+        early_outs = {}
+
+        def early_products(us, b):
+            early_bank = psum.tile([P, 2, HALF, FEAT], F32, tag="x1_bank", bufs=X1_BANKS)
+            for j in range(2):
+                for v in range(HALF):
+                    nc.tensor.matmul_mx(
+                        out=early_bank[:, j, v, :],
+                        lhsT=s_codes[:, us.start + v, :].bitcast(FP8X4),
+                        lhsT_scale=s_scales[:, us.start + v, :],
+                        rhs=x_codes[:, b + j, :].bitcast(FP8X4),
+                        rhs_scale=x_scales[:, b + j, :],
+                        start=True,
+                        stop=True,
+                    )
+            if b not in early_outs:
+                early_out = stage.tile([P, 2, PACK, FEAT], F32, bufs=EARLY // 2)
+                early_outs[b] = early_out
+            nc.scalar.copy(out=early_outs[b][:, :, us, :], in_=early_bank[:])
+            nc.sync.dma_start(
+                out=out_0[b : b + 2].rearrange("b (q u) d -> q b u d", u=PACK)[:, :, us, :], in_=early_outs[b][:, :, us, :]
+            )
 
         def first_product(b):
-            x1_bank = psum.tile([P, PACK, FEAT], F32, bufs=X1_BANKS)
+            x1_bank = psum.tile([P, PACK, FEAT], F32, tag="x1_bank", bufs=X1_BANKS)
             multiply_by_support(x1_bank, x_codes[:, b, :], x_scales[:, b, :])
             x1_banks[b] = x1_bank
 
         def take_x1(b):
             x1_bank = x1_banks[b]
-            x1_out = stage.tile([P, PACK, FEAT], F32)
-            nc.scalar.copy(out=x1_out[:], in_=x1_bank[:])
-            nc.sync.dma_start(out=out_0[b].rearrange("(q u) d -> q u d", u=PACK), in_=x1_out[:])
-            nc.scalar.copy(out=x1_grouped[:, b], in_=x1_bank[:].rearrange("q u d -> q d u"))
+            for step in ("group", "store") if b >= BATCH - X1_QUANT else ("store", "group"):
+                if step == "store":
+                    x1_out = stage.tile([P, PACK, FEAT], F32)
+                    nc.scalar.copy(out=x1_out[:], in_=x1_bank[:])
+                    nc.sync.dma_start(out=out_0[b].rearrange("(q u) d -> q u d", u=PACK), in_=x1_out[:])
+                else:
+                    nc.scalar.copy(out=x1_grouped[:, b], in_=x1_bank[:].rearrange("q u d -> q d u"))
 
         x2_banks = {}
 
@@ -169,27 +205,39 @@ def tile_dgcn_pa_t_kernel(tc, inputs, adj, out_0, out_1):
             )
             nc.sync.dma_start(out=out_1[b].rearrange("(q u) d -> q u d", u=PACK), in_=x2_out[:])
 
-        for b in range(SCALAR_X):
+        first_half = slice(0, HALF)
+        second_half = slice(HALF, PACK)
+        for b in range(EARLY):
             regroup_x(nc.scalar.copy, b)
-        quantise(x_codes, x_scales, x_grouped, 0, X_QUANT // 2)
-        nc.vector.quantize_mx(
-            out=s_codes[:].rearrange("p u q -> p (u q)").bitcast(FP8X4),
-            scales=s_scales[:].rearrange("p u q -> p (u q)"),
-            in_=s_grouped[:].rearrange("p u q t -> p (u q t)"),
-        )
-        quantise(x_codes, x_scales, x_grouped, X_QUANT // 2, X_QUANT // 2)
+        scale_columns(first_half)
+        quantise(x_codes, x_scales, x_grouped, 0, 2)
+        quantise_support(first_half)
+        early_products(first_half, 0)
+        quantise(x_codes, x_scales, x_grouped, 2, 2)
+        early_products(first_half, 2)
+        for b in range(EARLY, SCALAR_X):
+            regroup_x(nc.scalar.copy, b)
+        scale_columns(second_half)
+        regroup_x(nc.vector.tensor_copy, SCALAR_X + 1)
+        quantise_support(second_half)
+        for b in range(0, EARLY, 2):
+            early_products(second_half, b)
+        regroup_x(nc.vector.tensor_copy, SCALAR_X)
+        regroup_x(nc.vector.tensor_copy, SCALAR_X + 2)
+        quantise(x_codes, x_scales, x_grouped, X_QUANT, X_QUANT)
         x1_groups = {}
         for b in range(0, BATCH - X1_QUANT, X1_QUANT):
             x1_groups[b + X1_QUANT - 1] = (b, X1_QUANT)
         for b in range(BATCH - X1_QUANT, BATCH):
             x1_groups[b] = (b, 1)
-        for b in range(AHEAD):
-            first_product(b)
-        for b in range(BATCH + OUT_LAG):
-            if b + AHEAD < BATCH:
+        for b in range(EARLY - AHEAD, BATCH + OUT_LAG):
+            if EARLY <= b + AHEAD < BATCH:
                 first_product(b + AHEAD)
-            if b < BATCH:
+            if EARLY <= b < BATCH:
                 take_x1(b)
+            if b == EARLY - 1:
+                for c in range(0, EARLY, 2):
+                    nc.vector.tensor_copy(out=x1_grouped[:, c : c + 2], in_=early_outs[c][:].rearrange("q b u d -> q b d u"))
             if b - QUANT_LAG in x1_groups:
                 first, count = x1_groups[b - QUANT_LAG]
                 quantise(x1_codes, x1_scales, x1_grouped, first, count)
@@ -197,7 +245,7 @@ def tile_dgcn_pa_t_kernel(tc, inputs, adj, out_0, out_1):
                     second_product(c)
             if b >= OUT_LAG:
                 finish_x2(b - OUT_LAG)
-            if b + SCALAR_X < BATCH:
-                regroup_x(nc.vector.tensor_copy, b + SCALAR_X)
-            if (b + SCALAR_X) % X_QUANT == 0 and X_QUANT < b + SCALAR_X <= BATCH:
-                quantise(x_codes, x_scales, x_grouped, b + SCALAR_X - X_QUANT, X_QUANT)
+            if b + SCALAR_X + 1 < BATCH:
+                regroup_x(nc.vector.tensor_copy, b + SCALAR_X + 1)
+            if (b + AHEAD + 1) % X_QUANT == 0 and 2 * X_QUANT <= b + AHEAD + 1 < BATCH:
+                quantise(x_codes, x_scales, x_grouped, b + AHEAD + 1, X_QUANT)

@@ -20,7 +20,7 @@ FLOPS = 2 * 2 * BATCH * NODES * NODES * FEAT
 
 LOAD_BATCHES = 4
 RUN = 4
-SCALAR_X = 6
+SCALAR_X = 5
 X_QUANT = 4
 X1_QUANT = 2
 AHEAD = 2
@@ -93,6 +93,8 @@ def tile_dgcn_pa_t_kernel(tc, inputs, adj, out_0, out_1):
         m_scaled = keep.tile([P, PACK, NODES], F32)
         for t in range(0, PACK, 2):
             nc.scalar.activation(out=m_scaled[:, t, :], in_=m[:, t, :], func=ACT.Copy, scale=dd[:, t : t + 1])
+        dd_last = keep.tile([P, P], F32)
+        nc.scalar.copy(out=dd_last[:], in_=dd_row[:, PACK - 1, :])
         for t in range(1, PACK, 2):
             nc.vector.tensor_scalar_mul(out=m_scaled[:, t, :], in0=m[:, t, :], scalar1=dd[:, t : t + 1])
         s_grouped = keep.tile([P, PACK, P, PACK], BF16, align_bytes=64)
@@ -103,9 +105,16 @@ def tile_dgcn_pa_t_kernel(tc, inputs, adj, out_0, out_1):
             nc.vector.tensor_tensor(
                 out=s_grouped[:, us],
                 in0=m_scaled[:].rearrange("p t (q u) -> p u q t", u=PACK)[:, us],
-                in1=dd_row[:, us].unsqueeze(3).to_broadcast([P, HALF, P, PACK]),
+                in1=dd_row[:, us].unsqueeze(3).to_broadcast([P, us.stop - us.start, P, PACK]),
                 op=ALU.mult,
             )
+
+        nc.gpsimd.tensor_tensor(
+            out=s_grouped[:, PACK - 1],
+            in0=m_scaled[:].rearrange("p t (q u) -> p u q t", u=PACK)[:, PACK - 1],
+            in1=dd_last[:].unsqueeze(2).to_broadcast([P, P, PACK]),
+            op=ALU.mult,
+        )
 
         def quantise_support(us):
             nc.vector.quantize_mx(
@@ -217,13 +226,13 @@ def tile_dgcn_pa_t_kernel(tc, inputs, adj, out_0, out_1):
         early_products(first_half, 2)
         for b in range(EARLY, SCALAR_X):
             regroup_x(nc.scalar.copy, b)
-        scale_columns(second_half)
-        regroup_x(nc.vector.tensor_copy, SCALAR_X + 1)
+        scale_columns(slice(HALF, PACK - 1))
+        regroup_x(nc.vector.tensor_copy, SCALAR_X)
         quantise_support(second_half)
         for b in range(0, EARLY, 2):
             early_products(second_half, b)
-        regroup_x(nc.vector.tensor_copy, SCALAR_X)
-        regroup_x(nc.vector.tensor_copy, SCALAR_X + 2)
+        for b in range(SCALAR_X + 1, 2 * X_QUANT + 1):
+            regroup_x(nc.vector.tensor_copy, b)
         quantise(x_codes, x_scales, x_grouped, X_QUANT, X_QUANT)
         x1_groups = {}
         for b in range(0, BATCH - X1_QUANT, X1_QUANT):
@@ -245,7 +254,7 @@ def tile_dgcn_pa_t_kernel(tc, inputs, adj, out_0, out_1):
                     second_product(c)
             if b >= OUT_LAG:
                 finish_x2(b - OUT_LAG)
-            if b + SCALAR_X + 1 < BATCH:
-                regroup_x(nc.vector.tensor_copy, b + SCALAR_X + 1)
+            if b + 2 * X_QUANT - 1 < BATCH:
+                regroup_x(nc.vector.tensor_copy, b + 2 * X_QUANT - 1)
             if (b + AHEAD + 1) % X_QUANT == 0 and 2 * X_QUANT <= b + AHEAD + 1 < BATCH:
                 quantise(x_codes, x_scales, x_grouped, b + AHEAD + 1, X_QUANT)

@@ -222,16 +222,15 @@ def tile_dgcn_pa_t_kernel(tc, inputs, adj, out_0, out_1):
         quantise(x_codes, x_scales, x_grouped, 0, 2)
         quantise_support(first_half)
         early_products(first_half, 0)
-        quantise(x_codes, x_scales, x_grouped, 2, 2)
-        early_products(first_half, 2)
         for b in range(EARLY, SCALAR_X):
             regroup_x(nc.scalar.copy, b)
         scale_columns(slice(HALF, PACK - 1))
-        regroup_x(nc.vector.tensor_copy, SCALAR_X)
+        quantise(x_codes, x_scales, x_grouped, 2, 2)
+        early_products(first_half, 2)
         quantise_support(second_half)
         for b in range(0, EARLY, 2):
             early_products(second_half, b)
-        for b in range(SCALAR_X + 1, 2 * X_QUANT + 1):
+        for b in range(SCALAR_X, 2 * X_QUANT + 1):
             regroup_x(nc.vector.tensor_copy, b)
         quantise(x_codes, x_scales, x_grouped, X_QUANT, X_QUANT)
         x1_groups = {}

@@ -93,8 +93,8 @@ def tile_dgcn_pa_t_kernel(tc, inputs, adj, out_0, out_1):
         m_scaled = keep.tile([P, PACK, NODES], F32)
         for t in range(0, PACK, 2):
             nc.scalar.activation(out=m_scaled[:, t, :], in_=m[:, t, :], func=ACT.Copy, scale=dd[:, t : t + 1])
-        dd_last = keep.tile([P, P], F32)
-        nc.scalar.copy(out=dd_last[:], in_=dd_row[:, PACK - 1, :])
+        dd_last = keep.tile([P, HALF, P], F32)
+        nc.scalar.copy(out=dd_last[:], in_=dd_row[:, HALF:PACK, :])
         for t in range(1, PACK, 2):
             nc.vector.tensor_scalar_mul(out=m_scaled[:, t, :], in0=m[:, t, :], scalar1=dd[:, t : t + 1])
         s_grouped = keep.tile([P, PACK, P, PACK], BF16, align_bytes=64)
@@ -112,7 +112,13 @@ def tile_dgcn_pa_t_kernel(tc, inputs, adj, out_0, out_1):
         nc.gpsimd.tensor_tensor(
             out=s_grouped[:, PACK - 1],
             in0=m_scaled[:].rearrange("p t (q u) -> p u q t", u=PACK)[:, PACK - 1],
-            in1=dd_last[:].unsqueeze(2).to_broadcast([P, P, PACK]),
+            in1=dd_last[:, HALF - 1].unsqueeze(2).to_broadcast([P, P, PACK]),
+            op=ALU.mult,
+        )
+        nc.gpsimd.tensor_tensor(
+            out=s_grouped[:, HALF, P // 2 :],
+            in0=m_scaled[:].rearrange("p t (q u) -> p u q t", u=PACK)[:, HALF, P // 2 :],
+            in1=dd_last[:, 0, P // 2 :].unsqueeze(2).to_broadcast([P, P // 2, PACK]),
             op=ALU.mult,
         )
 
@@ -224,7 +230,12 @@ def tile_dgcn_pa_t_kernel(tc, inputs, adj, out_0, out_1):
         early_products(first_half, 0)
         for b in range(EARLY, SCALAR_X):
             regroup_x(nc.scalar.copy, b)
-        scale_columns(slice(HALF, PACK - 1))
+        nc.vector.tensor_tensor(
+            out=s_grouped[:, HALF, : P // 2],
+            in0=m_scaled[:].rearrange("p t (q u) -> p u q t", u=PACK)[:, HALF, : P // 2],
+            in1=dd_row[:, HALF, : P // 2].unsqueeze(2).to_broadcast([P, P // 2, PACK]),
+            op=ALU.mult,
+        )
         quantise(x_codes, x_scales, x_grouped, 2, 2)
         early_products(first_half, 2)
         quantise_support(second_half)

from contextlib import ExitStack

import concourse.mybir as mybir
from concourse.masks import make_identity

F32 = mybir.dt.float32
BF16 = mybir.dt.bfloat16
U32 = mybir.dt.uint32
U8 = mybir.dt.uint8
FP8X4 = mybir.dt.float8_e4m3fn_x4
ALU = mybir.AluOpType
ACT = mybir.ActivationFunctionType

P = 128
PACK = 4
BATCH = 16
NODES = P * PACK
FEAT = 128
FLOPS = 2 * 2 * BATCH * NODES * NODES * FEAT

LOAD_BATCHES = 4
RUN = 4
SCALAR_X = 5
X_QUANT = 4
X1_QUANT = 2
AHEAD = 2
QUANT_LAG = 2
OUT_LAG = 4
EARLY = 4
HALF = PACK // 2
X1_BANKS = 4
X2_BANKS = 3
STAGE_BUFS = 8


def tile_dgcn_pa_t_kernel(tc, inputs, adj, out_0, out_1):
    nc = tc.nc
    with ExitStack() as ctx:
        ctx.enter_context(tc.manual_schedule())
        keep = ctx.enter_context(tc.tile_pool(name="keep", bufs=1))
        stage = ctx.enter_context(tc.tile_pool(name="stage", bufs=STAGE_BUFS))
        psum = ctx.enter_context(tc.psum_pool(name="psum", bufs=1))

        adj_raw = keep.tile([P, PACK, NODES], BF16)
        adj_rows = adj.rearrange("(p t) i -> p t i", t=PACK)
        for t in range(PACK):
            nc.sync.dma_start(out=adj_raw[:, t, :], in_=adj_rows[:, t, :])
        x_raw = keep.tile([P, BATCH, PACK, FEAT], BF16)
        for b in range(0, BATCH, LOAD_BATCHES):
            nc.sync.dma_start(
                out=x_raw[:, b : b + LOAD_BATCHES],
                in_=inputs[b : b + LOAD_BATCHES].rearrange("b (p t) d -> p b t d", t=PACK),
            )

        one = keep.tile([P, 1], F32)
        nc.vector.memset(one[:], 1.0)
        warm = keep.tile([P, 1], F32)
        nc.scalar.activation(out=warm[:], in_=one[:], func=ACT.Abs_reciprocal_sqrt)

        ident = keep.tile([P, P], F32)
        make_identity(nc, ident[:])
        eye = keep.tile([P, PACK, P, PACK], BF16)
        nc.vector.memset(eye[:], 0.0)
        for t in range(PACK):
            nc.vector.tensor_copy(out=eye[:, t, :, t], in_=ident[:])

        m = keep.tile([P, PACK, NODES], F32)
        row_sum = keep.tile([P, PACK], F32)
        unused = keep.tile([P, NODES], BF16)
        for t in range(0, PACK, 2):
            nc.vector.scalar_tensor_tensor(
                out=m[:, t, :],
                in0=adj_raw[:, t, :],
                scalar=1.0,
                in1=eye[:, t].rearrange("p q u -> p (q u)"),
                op0=ALU.mult,
                op1=ALU.add,
                accum_out=row_sum[:, t : t + 1],
            )
        for t in range(1, PACK, 2):
            nc.scalar.activation(
                out=unused[:], in_=adj_raw[:, t, :], func=ACT.Copy, bias=1.0 / NODES, accum_out=row_sum[:, t : t + 1]
            )
        dd = keep.tile([P, PACK], F32)
        nc.scalar.activation(out=dd[:], in_=row_sum[:], func=ACT.Abs_reciprocal_sqrt)
        for t in range(1, PACK, 2):
            nc.vector.tensor_tensor(
                out=m[:, t, :], in0=adj_raw[:, t, :], in1=eye[:, t].rearrange("p q u -> p (q u)"), op=ALU.add
            )
        dd_row = psum.tile([P, PACK, P], F32)
        for u in range(PACK):
            nc.tensor.transpose(dd_row[:, u, :], dd[:, u : u + 1].to_broadcast([P, P]), ident[:])
        m_scaled = keep.tile([P, PACK, NODES], F32)
        for t in range(0, PACK, 2):
            nc.scalar.activation(out=m_scaled[:, t, :], in_=m[:, t, :], func=ACT.Copy, scale=dd[:, t : t + 1])
        dd_last = keep.tile([P, HALF, P], F32)
        nc.scalar.copy(out=dd_last[:], in_=dd_row[:, HALF:PACK, :])
        for t in range(1, PACK, 2):
            nc.vector.tensor_scalar_mul(out=m_scaled[:, t, :], in0=m[:, t, :], scalar1=dd[:, t : t + 1])
        s_grouped = keep.tile([P, PACK, P, PACK], BF16, align_bytes=64)
        s_codes = keep.tile([P, PACK, P], U32, align_bytes=64)
        s_scales = keep.tile([P, PACK, P], U8, align_bytes=64)

        def scale_columns(us):
            nc.vector.tensor_tensor(
                out=s_grouped[:, us],
                in0=m_scaled[:].rearrange("p t (q u) -> p u q t", u=PACK)[:, us],
                in1=dd_row[:, us].unsqueeze(3).to_broadcast([P, us.stop - us.start, P, PACK]),
                op=ALU.mult,
            )

        nc.gpsimd.tensor_tensor(
            out=s_grouped[:, PACK - 1],
            in0=m_scaled[:].rearrange("p t (q u) -> p u q t", u=PACK)[:, PACK - 1],
            in1=dd_last[:, HALF - 1].unsqueeze(2).to_broadcast([P, P, PACK]),
            op=ALU.mult,
        )
        nc.gpsimd.tensor_tensor(
            out=s_grouped[:, HALF, P // 2 :],
            in0=m_scaled[:].rearrange("p t (q u) -> p u q t", u=PACK)[:, HALF, P // 2 :],
            in1=dd_last[:, 0, P // 2 :].unsqueeze(2).to_broadcast([P, P // 2, PACK]),
            op=ALU.mult,
        )

        def quantise_support(us):
            nc.vector.quantize_mx(
                out=s_codes[:, us].rearrange("p u q -> p (u q)").bitcast(FP8X4),
                scales=s_scales[:, us].rearrange("p u q -> p (u q)"),
                in_=s_grouped[:, us].rearrange("p u q t -> p (u q t)"),
            )

        x_grouped = keep.tile([P, BATCH, FEAT, PACK], BF16, align_bytes=64)
        x_codes = keep.tile([P, BATCH, FEAT], U32, align_bytes=64)
        x_scales = keep.tile([P, BATCH, FEAT], U8, align_bytes=64)

        def regroup_x(copy, b):
            copy(
                out=x_grouped[:, b].rearrange("p (c i) t -> p c t i", i=RUN),
                in_=x_raw[:, b].rearrange("p t (c i) -> p c t i", i=RUN),
            )

        def quantise(codes, scales, grouped, b, count):
            nc.vector.quantize_mx(
                out=codes[:, b : b + count, :].rearrange("p b d -> p (b d)").bitcast(FP8X4),
                scales=scales[:, b : b + count, :].rearrange("p b d -> p (b d)"),
                in_=grouped[:, b : b + count].rearrange("p b d t -> p (b d t)"),
            )

        x1_grouped = keep.tile([P, BATCH, FEAT, PACK], BF16, align_bytes=64)
        x1_codes = keep.tile([P, BATCH, FEAT], U32, align_bytes=64)
        x1_scales = keep.tile([P, BATCH, FEAT], U8, align_bytes=64)

        def multiply_by_support(bank, codes, scales):
            for u in range(PACK):
                nc.tensor.matmul_mx(
                    out=bank[:, u, :],
                    lhsT=s_codes[:, u, :].bitcast(FP8X4),
                    lhsT_scale=s_scales[:, u, :],
                    rhs=codes.bitcast(FP8X4),
                    rhs_scale=scales,
                    start=True,
                    stop=True,
                )

        x1_banks = {}
        early_outs = {}

        def early_products(us, b):
            early_bank = psum.tile([P, 2, HALF, FEAT], F32, tag="x1_bank", bufs=X1_BANKS)
            for j in range(2):
                for v in range(HALF):
                    nc.tensor.matmul_mx(
                        out=early_bank[:, j, v, :],
                        lhsT=s_codes[:, us.start + v, :].bitcast(FP8X4),
                        lhsT_scale=s_scales[:, us.start + v, :],
                        rhs=x_codes[:, b + j, :].bitcast(FP8X4),
                        rhs_scale=x_scales[:, b + j, :],
                        start=True,
                        stop=True,
                    )
            if b not in early_outs:
                early_out = stage.tile([P, 2, PACK, FEAT], F32, bufs=EARLY // 2)
                early_outs[b] = early_out
            nc.scalar.copy(out=early_outs[b][:, :, us, :], in_=early_bank[:])
            nc.sync.dma_start(
                out=out_0[b : b + 2].rearrange("b (q u) d -> q b u d", u=PACK)[:, :, us, :], in_=early_outs[b][:, :, us, :]
            )

        def first_product(b):
            x1_bank = psum.tile([P, PACK, FEAT], F32, tag="x1_bank", bufs=X1_BANKS)
            multiply_by_support(x1_bank, x_codes[:, b, :], x_scales[:, b, :])
            x1_banks[b] = x1_bank

        def take_x1(b):
            x1_bank = x1_banks[b]
            for step in ("group", "store") if b >= BATCH - X1_QUANT else ("store", "group"):
                if step == "store":
                    x1_out = stage.tile([P, PACK, FEAT], F32)
                    nc.scalar.copy(out=x1_out[:], in_=x1_bank[:])
                    nc.sync.dma_start(out=out_0[b].rearrange("(q u) d -> q u d", u=PACK), in_=x1_out[:])
                else:
                    nc.scalar.copy(out=x1_grouped[:, b], in_=x1_bank[:].rearrange("q u d -> q d u"))

        x2_banks = {}

        def second_product(b):
            x2_bank = psum.tile([P, PACK, FEAT], F32, bufs=X2_BANKS)
            multiply_by_support(x2_bank, x1_codes[:, b, :], x1_scales[:, b, :])
            x2_banks[b] = x2_bank

        def finish_x2(b):
            x2_out = stage.tile([P, PACK, FEAT], F32)
            nc.vector.scalar_tensor_tensor(
                out=x2_out[:],
                in0=x2_banks[b][:],
                scalar=2.0,
                in1=x_raw[:, b],
                op0=ALU.mult,
                op1=ALU.subtract,
            )
            nc.sync.dma_start(out=out_1[b].rearrange("(q u) d -> q u d", u=PACK), in_=x2_out[:])

        first_half = slice(0, HALF)
        second_half = slice(HALF, PACK)
        for b in range(EARLY):
            regroup_x(nc.scalar.copy, b)
        scale_columns(first_half)
        quantise(x_codes, x_scales, x_grouped, 0, 2)
        quantise_support(first_half)
        early_products(first_half, 0)
        for b in range(EARLY, SCALAR_X):
            regroup_x(nc.scalar.copy, b)
        nc.vector.tensor_tensor(
            out=s_grouped[:, HALF, : P // 2],
            in0=m_scaled[:].rearrange("p t (q u) -> p u q t", u=PACK)[:, HALF, : P // 2],
            in1=dd_row[:, HALF, : P // 2].unsqueeze(2).to_broadcast([P, P // 2, PACK]),
            op=ALU.mult,
        )
        quantise(x_codes, x_scales, x_grouped, 2, 2)
        early_products(first_half, 2)
        quantise_support(second_half)
        for b in range(0, EARLY, 2):
            early_products(second_half, b)
        for b in range(SCALAR_X, 2 * X_QUANT + 1):
            regroup_x(nc.vector.tensor_copy, b)
        quantise(x_codes, x_scales, x_grouped, X_QUANT, X_QUANT)
        x1_groups = {}
        for b in range(0, BATCH - X1_QUANT, X1_QUANT):
            x1_groups[b + X1_QUANT - 1] = (b, X1_QUANT)
        for b in range(BATCH - X1_QUANT, BATCH):
            x1_groups[b] = (b, 1)
        for b in range(EARLY - AHEAD, BATCH + OUT_LAG):
            if EARLY <= b + AHEAD < BATCH:
                first_product(b + AHEAD)
            if EARLY <= b < BATCH:
                take_x1(b)
            if b == EARLY - 1:
                for c in range(0, EARLY, 2):
                    nc.vector.tensor_copy(out=x1_grouped[:, c : c + 2], in_=early_outs[c][:].rearrange("q b u d -> q b d u"))
            if b - QUANT_LAG in x1_groups:
                first, count = x1_groups[b - QUANT_LAG]
                quantise(x1_codes, x1_scales, x1_grouped, first, count)
                for c in range(first, first + count):
                    second_product(c)
            if b >= OUT_LAG:
                finish_x2(b - OUT_LAG)
            if b + 2 * X_QUANT - 1 < BATCH:
                regroup_x(nc.vector.tensor_copy, b + 2 * X_QUANT - 1)
            if (b + AHEAD + 1) % X_QUANT == 0 and 2 * X_QUANT <= b + AHEAD + 1 < BATCH:
                quantise(x_codes, x_scales, x_grouped, b + AHEAD + 1, X_QUANT)
